import numpy as np
import ml_dtypes


def mxq(x, axis, fmt="e4m3"):
    dtype, down = {"e4m3": (ml_dtypes.float8_e4m3fn, 7), "e5m2": (ml_dtypes.float8_e5m2, 14)}[fmt]
    v = np.moveaxis(np.asarray(x, np.float32).astype(ml_dtypes.bfloat16).astype(np.float64), axis, -1)
    blocks = v.reshape(v.shape[:-1] + (-1, 32))
    amax = np.abs(blocks).max(-1, keepdims=True)
    byte = np.maximum(np.where(amax > 0, np.frexp(amax)[1] - 1 + 127, 0) - down, 1)
    scale = np.exp2(byte - 127.0)
    codes = (blocks / scale).astype(np.float32).astype(dtype).astype(np.float64)
    return np.moveaxis((codes * scale).reshape(v.shape), -1, axis)


WIDE = False


def mx_kscale(k):
    if not WIDE:
        return np.ones(k)
    levels = np.array([10, -10, 5, -5, 0])
    if k % 512:
        return np.exp2(np.random.permutation(np.resize(levels, k // 32))).repeat(32)
    a = np.empty((k // 512, 16))
    for p in range(k // 512):
        a[p, :8] = np.random.permutation(np.resize(levels, 8))
        for g in range(8):
            far = levels[np.abs(levels - a[p, g]) >= 10]
            a[p, g + 8] = far[np.random.randint(len(far))]
    return np.exp2(a.ravel()).repeat(32)


BF16 = ml_dtypes.bfloat16


def bf(x):
    return np.asarray(x, np.float32).astype(BF16)


def f64(x):
    return np.asarray(x).astype(np.float64)


B, F, H, W, P, DIN, DIM, HEADS = 1, 6, 8, 24, 64, 1536, 1536, 12
S = F * H * W
HD = DIM // HEADS
C = HD // 2
T1 = C // 3
T0 = C - 2 * T1
EPS = 1e-6


def rmsnorm(v, g):
    return v * (1.0 / np.sqrt(np.mean(v * v, axis=-1, keepdims=True) + EPS)) * g


def rope(v, theta):
    ang = np.concatenate([
        np.broadcast_to(theta[:F, :T0][:, None, None, :], (F, H, W, T0)),
        np.broadcast_to(theta[:H, T0:T0 + T1][None, :, None, :], (F, H, W, T1)),
        np.broadcast_to(theta[:W, T0 + T1:T0 + 2 * T1][None, None, :, :], (F, H, W, T1)),
    ], axis=-1).reshape(S, C)[None, :, None, :]
    cos, sin = np.cos(ang), np.sin(ang)
    vp = v.reshape(B, S, HEADS, C, 2)
    vr, vi = vp[..., 0], vp[..., 1]
    return np.stack([vr * cos - vi * sin, vr * sin + vi * cos], axis=-1).reshape(B, S, HEADS, HD)


def draw0():
    s = mx_kscale(DIN)
    return {
        "x": bf(np.random.standard_normal((B, S, DIN)) * s),
        "theta": bf(np.random.random_sample((P, C)) * 2.0 * np.pi),
        "wq": bf(np.random.standard_normal((DIM, DIN)) / np.sqrt(DIN) / s[None, :]),
        "bq": bf(np.random.standard_normal(DIM) * 0.2),
        "wk": bf(np.random.standard_normal((DIM, DIN)) / np.sqrt(DIN) / s[None, :]),
        "bk": bf(np.random.standard_normal(DIM) * 0.2),
        "gq": bf(1.0 + 0.1 * np.random.standard_normal(DIM)),
        "gk": bf(1.0 + 0.1 * np.random.standard_normal(DIM)),
    }


def core(x, theta, wq, bq, wk, bk, gq, gk):
    xq = mxq(f64(x), 2, "e4m3")
    th = f64(theta)
    q = rmsnorm((xq @ mxq(f64(wq), 1, "e4m3").T) + f64(bq), f64(gq))
    k = rmsnorm((xq @ mxq(f64(wk), 1, "e4m3").T) + f64(bk), f64(gk))
    return rope(q, th), rope(k, th)


def e4m3fn_bytes(y):
    return np.clip(np.asarray(y, np.float64), -448.0, 448.0).astype(np.float32).astype(ml_dtypes.float8_e4m3fn).view(np.uint8)


def e4m3fn_values(b):
    return np.asarray(b, np.uint8).view(ml_dtypes.float8_e4m3fn).astype(np.float64)


def setup_inputs():
    d = draw0()
    x0 = np.asarray(d['wq']).astype(np.float64)
    s = (np.max(np.abs(x0), axis=(0,), keepdims=True) / 448.0).astype(np.float32)
    out = {}
    for k, v in d.items():
        if k == 'wq':
            out['wq_bytes'] = e4m3fn_bytes(x0 / s.astype(np.float64))
            out['wq_scale'] = s
        else:
            out[k] = v
    return out


def reference(x, theta, wq_bytes, wq_scale, bq, wk, bk, gq, gk):
    return core(x, theta, e4m3fn_values(wq_bytes) * wq_scale.astype(np.float64), bq, wk, bk, gq, gk)

@@ -1,0 +1,439 @@
+from contextlib import ExitStack
+import math
+
+import concourse.mybir as mybir
+from concourse.masks import make_identity
+
+F32 = mybir.dt.float32
+BF16 = mybir.dt.bfloat16
+U32 = mybir.dt.uint32
+U8 = mybir.dt.uint8
+I32 = mybir.dt.int32
+FP8 = mybir.dt.float8_e4m3fn
+FP8X4 = mybir.dt.float8_e4m3fn_x4
+ALU = mybir.AluOpType
+ACT = mybir.ActivationFunctionType
+
+P = 128
+TOKENS = 1152
+TOKEN_TILES = TOKENS // P
+K = 1536
+CH = 1536
+HEADS = CH // P
+PASSES = K // (4 * P)
+WORDS = 2 * P
+FRAMES, HEIGHT, WIDTH = 6, 8, 24
+PAIRS = 64
+BY_FRAME, BY_HEIGHT = 22, 21
+ROW_H, ROW_W = FRAMES, FRAMES + HEIGHT
+EPS = 1e-6
+PI_BELOW = 3.1415925
+FLOPS = 2 * TOKENS * K * 2 * CH
+
+Q, KEY = 0, 1
+UNITS = ((KEY, 0, 3), (KEY, 3, 3), (KEY, 6, 3), (Q, 0, 3), (Q, 3, 3), (Q, 6, 2), (Q, 8, 1))
+UNIT_WIDTH = 3 * P
+COLUMN_GROUPS = {3: ((0, 256), (256, 128)), 2: ((0, 256),), 1: ((0, 128),)}
+STEP_HEADS = 3
+STEPS = HEADS // STEP_HEADS
+BANK_HEADS = 4
+BANKS = HEADS // BANK_HEADS
+ROPE_BANKS = (2, 2, 3, 2)
+ROW_PAIRS = CH // (2 * P)
+HALF = K // 2
+WIDEN_BESIDE = (1, 1, 0)
+VECTOR_ADDS = 3
+
+
+def tile_mpselfattentiontorch_pa_kernel(
+    tc, x, theta, wq_bytes, wq_scale, bq, wk, bk, gq, gk, out_0, out_1
+):
+    nc = tc.nc
+    outs = (out_0, out_1)
+    x_rows = x.flatten_outer_dims()
+
+    with ExitStack() as ctx:
+        ctx.enter_context(tc.manual_schedule(engines={mybir.EngineType.PE, mybir.EngineType.DVE}))
+        const = ctx.enter_context(tc.tile_pool(name="const", bufs=1))
+        bytes_pool = ctx.enter_context(tc.tile_pool(name="bytes", bufs=2))
+        wide_pool = ctx.enter_context(tc.tile_pool(name="wide", bufs=ROW_PAIRS))
+        grouped_pool = ctx.enter_context(tc.tile_pool(name="grouped", bufs=3))
+        heads_pool = ctx.enter_context(tc.tile_pool(name="heads", bufs=1))
+        mx_psum = ctx.enter_context(tc.psum_pool(name="mx_psum", bufs=3))
+        back_psum = ctx.enter_context(tc.psum_pool(name="back_psum", bufs=3))
+        turn_psum = ctx.enter_context(tc.psum_pool(name="turn_psum", bufs=2))
+
+        ident_f32 = const.tile([P, P], F32, name="ident_f32")
+        ident_bf16 = const.tile([P, P], BF16, name="ident_bf16")
+        vectors = const.tile([P, P], BF16, name="vectors")
+        per_channel = const.tile([P, 4 * HEADS], F32, name="per_channel")
+        bias_gain = const.tile([P, 2 * HEADS], F32, name="bias_gain")
+        angle_rows = const.tile([P, PAIRS], BF16, name="angle_rows")
+        trig = const.tile([P, TOKEN_TILES, 2 * P], F32, name="trig")
+        scale_rows = const.tile([P, K], F32, name="scale_rows")
+        x_codes = const.tile([P, PASSES, TOKENS], U32, name="x_codes", align_bytes=64)
+        x_scales = const.tile([P, PASSES, TOKENS], U8, name="x_scales", align_bytes=64)
+        w_codes = (
+            const.tile([P, PASSES, CH], U32, name="wq_codes", align_bytes=64),
+            const.tile([P, PASSES, CH], U32, name="wk_codes", align_bytes=64),
+        )
+        w_scales = (
+            const.tile([P, PASSES, CH], U8, name="wq_scales", align_bytes=64),
+            const.tile([P, PASSES, CH], U8, name="wk_scales", align_bytes=64),
+        )
+
+        turned = [0]
+        first_unit = [True]
+
+        def turn_bank(rows, tiles, g, codes, scales, col0, share):
+            n = tiles * P
+            if first_unit[0] and turned[0] % 5 >= 2:
+                bank = back_psum.tile([P, 4 * P], F32, name="turn_bank2", tag="back")
+            else:
+                bank = turn_psum.tile([P, 4 * P], F32, name="turn_bank", tag="turn")
+            for t in range(tiles):
+                words = rows[:, t, :].bitcast(F32)
+                for u in range(2):
+                    c = (2 * t + u) * P
+                    nc.tensor.transpose(
+                        bank[:, c : c + P], words[:, WORDS * g + u : WORDS * (g + 1) : 2], ident_f32[:]
+                    )
+            grouped = grouped_pool.tile([P, 8 * P], BF16, name="grouped", tag="grouped", align_bytes=64)
+            dst = grouped[:, 0 : 4 * n].bitcast(F32).rearrange("p (t r u) -> p t r u", t=tiles, u=2)
+            src = bank[:, 0 : 2 * n].rearrange("p (t u r) -> p t r u", t=tiles, u=2)
+            if share and turned[0] % 2 == 1:
+                nc.vector.tensor_copy(out=dst, in_=src)
+            else:
+                nc.scalar.copy(out=dst, in_=src)
+            turned[0] += 1
+            return (codes, scales, g, col0, n, grouped)
+
+        def quantise(job):
+            codes, scales, g, col0, n, grouped = job
+            nc.vector.quantize_mx(
+                out=codes[:, g, col0 : col0 + n].bitcast(FP8X4),
+                scales=scales[:, g, col0 : col0 + n],
+                in_=grouped[:, 0 : 4 * n],
+            )
+
+        wq_raw = {}
+        wq_wide = {}
+        widened = [0]
+
+        def load_bytes(j):
+            wq_raw[j] = bytes_pool.tile([P, 2, K], U8, name="wq_raw", tag="wq_raw")
+            nc.sync.dma_start(
+                out=wq_raw[j][:], in_=wq_bytes[2 * P * j : 2 * P * (j + 1), :].rearrange("(t p) k -> p t k", p=P)
+            )
+
+        def widen(count):
+            upto = min(widened[0] + count, 4 * ROW_PAIRS)
+            for i in range(widened[0], upto):
+                j, t, half = i // 4, (i // 2) % 2, i % 2
+                if i % 4 == 0:
+                    wq_wide[j] = wide_pool.tile([P, 2, K], BF16, name="wq_wide", tag="wq_wide")
+                cols = slice(half * HALF, (half + 1) * HALF)
+                nc.vector.tensor_tensor(
+                    out=wq_wide[j][:, t, cols],
+                    in0=wq_raw[j][:, t, cols].bitcast(FP8),
+                    in1=scale_rows[:, cols],
+                    op=ALU.mult,
+                )
+                if i % 4 == 3 and j + 2 < ROW_PAIRS:
+                    load_bytes(j + 2)
+            widened[0] = upto
+
+        def turn(rows, tiles, codes, scales, col0, share, beside):
+            waiting = None
+            for g in range(PASSES):
+                job = turn_bank(rows, tiles, g, codes, scales, col0, share)
+                if waiting is not None:
+                    quantise(waiting)
+                waiting = job
+                widen(beside[g])
+            quantise(waiting)
+
+        gained = {}
+        squared = {}
+
+        def project(n, h):
+            proj, tile0, tiles = UNITS[n]
+            width = tiles * P
+            acc = mx_psum.tile([P, 4 * P], F32, name="acc", tag="acc")
+            chans = slice(h * P, (h + 1) * P)
+            for c0, cols in COLUMN_GROUPS[tiles]:
+                toks = slice(tile0 * P + c0, tile0 * P + c0 + cols)
+                for g in range(PASSES):
+                    nc.tensor.matmul_mx(
+                        out=acc[:, c0 : c0 + cols],
+                        lhsT=w_codes[proj][:, g, chans].bitcast(FP8X4),
+                        lhsT_scale=w_scales[proj][:, g, chans],
+                        rhs=x_codes[:, g, toks].bitcast(FP8X4),
+                        rhs_scale=x_scales[:, g, toks],
+                        start=(g == 0),
+                        stop=(g == PASSES - 1),
+                    )
+            c = proj * HEADS + h
+            gained[(n, h)] = heads_pool.tile([P, UNIT_WIDTH], F32, name="gained", tag="gained", bufs=2 * HEADS)
+            squared[(n, h)] = heads_pool.tile(
+                [P, UNIT_WIDTH], F32, name="squared", tag="squared", bufs=HEADS + STEP_HEADS + 1
+            )
+            nc.scalar.activation(
+                out=gained[(n, h)][:, 0:width],
+                in_=acc[:, 0:width],
+                func=ACT.Identity,
+                bias=bias_gain[:, c : c + 1],
+                scale=per_channel[:, 2 * HEADS + c : 2 * HEADS + c + 1],
+            )
+            nc.scalar.activation(
+                out=squared[(n, h)][:, 0:width], in_=acc[:, 0:width], func=ACT.Square, bias=per_channel[:, c : c + 1]
+            )
+
+        with ExitStack() as early:
+            rows_pool = early.enter_context(tc.tile_pool(name="rows", bufs=4))
+            setup = early.enter_context(tc.tile_pool(name="setup", bufs=1))
+
+            def load_rows(dram, row0, tiles):
+                rows = rows_pool.tile([P, 2, K], BF16, name="rows", tag="rows")
+                nc.sync.dma_start(
+                    out=rows[:, 0:tiles, :],
+                    in_=dram[row0 : row0 + tiles * P, :].rearrange("(t p) k -> p t k", p=P),
+                )
+                return rows
+
+            nc.vector.memset(vectors[:], 0.0)
+            nc.vector.memset(angle_rows[:], 0.0)
+            for i, v in enumerate((bq, bk, gq, gk)):
+                nc.scalar.dma_start(
+                    out=vectors[HEADS * i : HEADS * (i + 1), :], in_=v.rearrange("(h c) -> h c", c=P)
+                )
+            nc.scalar.dma_start(out=angle_rows[0:FRAMES, 0:BY_FRAME], in_=theta[0:FRAMES, 0:BY_FRAME])
+            nc.scalar.dma_start(
+                out=angle_rows[ROW_H:ROW_W, BY_FRAME : BY_FRAME + BY_HEIGHT],
+                in_=theta[0:HEIGHT, BY_FRAME : BY_FRAME + BY_HEIGHT],
+            )
+            nc.scalar.dma_start(
+                out=angle_rows[ROW_W : ROW_W + WIDTH, BY_FRAME + BY_HEIGHT : PAIRS],
+                in_=theta[0:WIDTH, BY_FRAME + BY_HEIGHT : PAIRS],
+            )
+            x_raw = {0: load_rows(x_rows, 0, 2), 1: load_rows(x_rows, 2 * P, 2)}
+            wk_raw = {0: load_rows(wk, 0, 2), 1: load_rows(wk, 2 * P, 2)}
+            nc.sync.dma_start(out=scale_rows[:], in_=wq_scale.rearrange("o k -> (o k)").partition_broadcast(P))
+            load_bytes(0)
+            load_bytes(1)
+            make_identity(nc, ident_f32[:])
+
+            diff_f = setup.tile([P, TOKENS], I32, name="diff_f", tag="scratch", bufs=2)
+            diff_h = setup.tile([P, TOKENS], I32, name="diff_h", tag="scratch", bufs=2)
+            nc.gpsimd.iota(diff_f[:], pattern=[[1, FRAMES], [0, HEIGHT * WIDTH]], base=0, channel_multiplier=-1)
+            nc.gpsimd.iota(
+                diff_h[:], pattern=[[0, FRAMES], [1, HEIGHT], [0, WIDTH]], base=ROW_H, channel_multiplier=-1
+            )
+            make_identity(nc, ident_bf16[:])
+            picks_f = setup.tile([P, TOKENS], BF16, name="picks_f")
+            picks_fh = setup.tile([P, TOKENS], BF16, name="picks_fh")
+            picks = setup.tile([P, TOKENS], BF16, name="picks")
+            nc.vector.tensor_scalar(out=picks_f[:], in0=diff_f[:], scalar1=0.0, scalar2=None, op0=ALU.is_equal)
+            diff_w = setup.tile([P, TOKENS], I32, name="diff_w", tag="scratch", bufs=2)
+            nc.gpsimd.iota(
+                diff_w[:], pattern=[[0, FRAMES * HEIGHT], [1, WIDTH]], base=ROW_W, channel_multiplier=-1
+            )
+            nc.vector.scalar_tensor_tensor(
+                out=picks_fh[:], in0=diff_h[:], scalar=0.0, in1=picks_f[:], op0=ALU.is_equal, op1=ALU.add
+            )
+            nc.vector.scalar_tensor_tensor(
+                out=picks[:], in0=diff_w[:], scalar=0.0, in1=picks_fh[:], op0=ALU.is_equal, op1=ALU.add
+            )
+
+            def make_trig():
+                shifted = setup.tile([P, TOKEN_TILES * PAIRS], F32, name="shifted")
+                folded = setup.tile([P, TOKEN_TILES * PAIRS], F32, name="folded")
+                for lo, hi in ((0, 8), (8, TOKEN_TILES)):
+                    angles = turn_psum.tile([P, 4 * P], F32, name="angles", tag="turn")
+                    for tile in range(lo, hi):
+                        nc.tensor.matmul(
+                            out=angles[:, (tile - lo) * PAIRS : (tile - lo + 1) * PAIRS],
+                            lhsT=picks[:, tile * P : (tile + 1) * P],
+                            rhs=angle_rows[:],
+                            start=True,
+                            stop=True,
+                        )
+                    nc.vector.tensor_scalar(
+                        out=shifted[:, lo * PAIRS : hi * PAIRS],
+                        in0=angles[:, 0 : (hi - lo) * PAIRS],
+                        scalar1=math.pi,
+                        scalar2=-PI_BELOW,
+                        op0=ALU.subtract,
+                        op1=ALU.max,
+                    )
+                nc.scalar.activation(out=folded[:], in_=shifted[:], func=ACT.Abs)
+                halves = trig[:].rearrange("p t (k j r) -> p t k j r", k=2, r=2)
+                for src, scale, bias, places in (
+                    (folded, 1.0, -0.5 * math.pi, (halves[:, :, 0, :, 0], halves[:, :, 0, :, 1])),
+                    (shifted, 1.0, 0.0, (halves[:, :, 1, :, 0],)),
+                    (shifted, -1.0, 0.0, (halves[:, :, 1, :, 1],)),
+                ):
+                    sines = setup.tile([P, TOKEN_TILES * PAIRS], F32, name="sines", tag="scratch", bufs=2)
+                    nc.scalar.activation(out=sines[:], in_=src[:], func=ACT.Sin, scale=scale, bias=bias)
+                    for place in places:
+                        nc.gpsimd.tensor_copy(out=place, in_=sines[:].rearrange("p (t j) -> p t j", j=PAIRS))
+
+            nothing = (0, 0, 0)
+            turn(x_raw[0], 2, x_codes, x_scales, 0, False, nothing)
+            wk_raw[2] = load_rows(wk, 4 * P, 2)
+            turn(x_raw[1], 2, x_codes, x_scales, 2 * P, False, nothing)
+            wk_raw[3] = load_rows(wk, 6 * P, 2)
+            turn(wk_raw[0], 2, w_codes[KEY], w_scales[KEY], 0, True, nothing)
+            wk_raw[4] = load_rows(wk, 8 * P, 2)
+
+            columns = turn_psum.tile([P, P], BF16, name="columns", tag="turn")
+            nc.tensor.transpose(columns[:], vectors[:], ident_bf16[:])
+            nc.vector.tensor_copy(out=per_channel[:], in_=columns[:, 0 : 4 * HEADS])
+            nc.vector.tensor_tensor(
+                out=bias_gain[:],
+                in0=per_channel[:, 0 : 2 * HEADS],
+                in1=per_channel[:, 2 * HEADS : 4 * HEADS],
+                op=ALU.mult,
+            )
+
+            for pair in range(ROW_PAIRS):
+                if pair + 1 < ROW_PAIRS:
+                    turn(wk_raw[pair + 1], 2, w_codes[KEY], w_scales[KEY], 2 * P * (pair + 1), True, WIDEN_BESIDE)
+                else:
+                    turn(x_raw[2], 2, x_codes, x_scales, 4 * P, True, WIDEN_BESIDE)
+                if pair == 0:
+                    wk_raw[5] = load_rows(wk, 10 * P, 2)
+                elif pair == 1:
+                    x_raw[2] = load_rows(x_rows, 4 * P, 2)
+                elif pair == 2:
+                    x_raw[3] = load_rows(x_rows, 6 * P, 2)
+                elif pair == 3:
+                    x_raw[4] = load_rows(x_rows, 8 * P, 1)
+                project(0, 2 * pair)
+                project(0, 2 * pair + 1)
+                if pair == 1:
+                    make_trig()
+            turn(x_raw[3], 2, x_codes, x_scales, 6 * P, True, WIDEN_BESIDE)
+            turn(x_raw[4], 1, x_codes, x_scales, 8 * P, True, WIDEN_BESIDE)
+
+        first_unit[0] = False
+        rope_pool = ctx.enter_context(tc.tile_pool(name="rope", bufs=4))
+        small = ctx.enter_context(tc.tile_pool(name="small", bufs=3))
+
+        scaled_trig = {}
+
+        def norm(n):
+            tile0, tiles = UNITS[n][1], UNITS[n][2]
+            sums = turn_psum.tile([P, 4 * P], F32, name="sums", tag="turn")
+            for t in range(tiles):
+                for h in range(HEADS):
+                    nc.tensor.matmul(
+                        out=sums[:, t * P : (t + 1) * P],
+                        lhsT=squared[(n, h)][:, t * P : (t + 1) * P],
+                        rhs=ident_f32[:],
+                        is_transpose=True,
+                        start=(h == 0),
+                        stop=(h == HEADS - 1),
+                    )
+            mean = small.tile([P, 4], F32, name="mean", tag="mean")
+            rstd = small.tile([P, 4], F32, name="rstd", tag="rstd")
+            for t in range(tiles):
+                unused = small.tile([P, P], F32, name="unused", tag="unused")
+                nc.scalar.activation(
+                    out=unused[:],
+                    in_=sums[:, t * P : (t + 1) * P],
+                    func=ACT.Identity,
+                    scale=1.0 / CH,
+                    bias=EPS / P,
+                    accum_out=mean[:, t : t + 1],
+                )
+            nc.scalar.activation(out=rstd[:, 0:tiles], in_=mean[:, 0:tiles], func=ACT.Abs_reciprocal_sqrt)
+            for t in range(tiles):
+                scaled_trig[(n, t)] = small.tile([P, 2 * P], F32, name="scaled_trig", tag="scaled_trig", bufs=8)
+                nc.scalar.activation(
+                    out=scaled_trig[(n, t)][:], in_=trig[:, tile0 + t, :], func=ACT.Copy, scale=rstd[:, t : t + 1]
+                )
+
+        banks = []
+        for n in range(len(UNITS)):
+            for t in range(UNITS[n][2]):
+                for b in range(BANKS):
+                    banks.append((n, t, b))
+        rotated = [0]
+        normed = [0]
+        added = [0]
+        products = []
+
+        def add_and_store():
+            proj, tile, b, straight, crossed = products.pop(0)
+            result = rope_pool.tile([P, 4 * P], F32, name="result", tag="result", bufs=6)
+            if added[0] >= len(banks) - VECTOR_ADDS and added[0] % 2 == 1:
+                nc.vector.tensor_tensor(out=result[:], in0=straight[:], in1=crossed[:], op=ALU.add)
+            else:
+                nc.gpsimd.tensor_tensor(out=result[:], in0=straight[:], in1=crossed[:], op=ALU.add)
+            added[0] += 1
+            nc.sync.dma_start(
+                out=outs[proj][0, tile * P : (tile + 1) * P, BANK_HEADS * b : BANK_HEADS * (b + 1), :].rearrange(
+                    "s h d -> s (h d)"
+                ),
+                in_=result[:],
+            )
+
+        def rotate(quota):
+            for i in range(rotated[0], min(rotated[0] + quota, normed[0])):
+                n, t, b = banks[i]
+                back = back_psum.tile([P, 4 * P], F32, name="back", tag="back")
+                for hh in range(BANK_HEADS):
+                    nc.tensor.transpose(
+                        back[:, hh * P : (hh + 1) * P],
+                        gained[(n, BANK_HEADS * b + hh)][:, t * P : (t + 1) * P],
+                        ident_f32[:],
+                    )
+                factors = scaled_trig[(n, t)]
+                straight = rope_pool.tile([P, 4 * P], F32, name="straight", tag="straight")
+                crossed = rope_pool.tile([P, 4 * P], F32, name="crossed", tag="crossed")
+                nc.vector.tensor_tensor(
+                    out=straight[:].rearrange("p (h c) -> p h c", h=BANK_HEADS),
+                    in0=back[:].rearrange("p (h c) -> p h c", h=BANK_HEADS),
+                    in1=factors[:, 0:P].unsqueeze(1).to_broadcast([P, BANK_HEADS, P]),
+                    op=ALU.mult,
+                )
+                nc.vector.tensor_tensor(
+                    out=crossed[:].rearrange("p (h j r) -> p h j r", h=BANK_HEADS, r=2),
+                    in0=back[:].rearrange("p (h j r) -> p h j r", h=BANK_HEADS, r=2)[:, :, :, ::-1],
+                    in1=factors[:, P : 2 * P]
+                    .rearrange("p (j r) -> p j r", r=2)
+                    .unsqueeze(1)
+                    .to_broadcast([P, BANK_HEADS, PAIRS, 2]),
+                    op=ALU.mult,
+                )
+                products.append((UNITS[n][0], UNITS[n][1] + t, b, straight, crossed))
+                if len(products) > 1:
+                    add_and_store()
+                rotated[0] += 1
+
+        wq_banks = PASSES * ROW_PAIRS
+        wq_steps = 2 * STEPS
+        wq_turned = 0
+        step = 0
+        for n in range(1, len(UNITS)):
+            for s in range(STEPS):
+                for h in range(STEP_HEADS * s, STEP_HEADS * (s + 1)):
+                    project(n, h)
+                rotate(ROPE_BANKS[s])
+                if s == 0:
+                    norm(n - 1)
+                    normed[0] += BANKS * UNITS[n - 1][2]
+                step += 1
+                due = min(wq_banks, (wq_banks * step + wq_steps - 1) // wq_steps)
+                for i in range(wq_turned, due):
+                    j, g = i // PASSES, i % PASSES
+                    widen(max(0, 4 * (j + 1) - widened[0]))
+                    quantise(turn_bank(wq_wide[j], 2, g, w_codes[Q], w_scales[Q], 2 * P * j, False))
+                    widen(1)
+                wq_turned = due
+        rotate(len(banks))
+        norm(len(UNITS) - 1)
+        normed[0] = len(banks)
+        rotate(len(banks))
+        add_and_store()

@@ -69,7 +69,7 @@ def tile_mpselfattentiontorch_pa_kernel(
         per_channel = const.tile([P, 4 * HEADS], F32, name="per_channel")
         bias_gain = const.tile([P, 2 * HEADS], F32, name="bias_gain")
         angle_rows = const.tile([P, PAIRS], BF16, name="angle_rows")
-        trig = const.tile([P, TOKEN_TILES, 2 * P], F32, name="trig")
+        trig = const.tile([P, TOKEN_TILES, 3 * PAIRS], F32, name="trig")
         scale_rows = const.tile([P, K], F32, name="scale_rows")
         x_codes = const.tile([P, PASSES, TOKENS], U32, name="x_codes", align_bytes=64)
         x_scales = const.tile([P, PASSES, TOKENS], U8, name="x_scales", align_bytes=64)
@@ -267,16 +267,16 @@ def tile_mpselfattentiontorch_pa_kernel(
                         op1=ALU.max,
                     )
                 nc.scalar.activation(out=folded[:], in_=shifted[:], func=ACT.Abs)
-                halves = trig[:].rearrange("p t (k j r) -> p t k j r", k=2, r=2)
-                for src, scale, bias, places in (
-                    (folded, 1.0, -0.5 * math.pi, (halves[:, :, 0, :, 0], halves[:, :, 0, :, 1])),
-                    (shifted, 1.0, 0.0, (halves[:, :, 1, :, 0],)),
-                    (shifted, -1.0, 0.0, (halves[:, :, 1, :, 1],)),
+                for plane, (src, scale, bias) in enumerate(
+                    ((folded, 1.0, -0.5 * math.pi), (shifted, 1.0, 0.0), (shifted, -1.0, 0.0))
                 ):
-                    sines = setup.tile([P, TOKEN_TILES * PAIRS], F32, name="sines", tag="scratch", bufs=2)
-                    nc.scalar.activation(out=sines[:], in_=src[:], func=ACT.Sin, scale=scale, bias=bias)
-                    for place in places:
-                        nc.gpsimd.tensor_copy(out=place, in_=sines[:].rearrange("p (t j) -> p t j", j=PAIRS))
+                    nc.scalar.activation(
+                        out=trig[:, :, plane * PAIRS : (plane + 1) * PAIRS],
+                        in_=src[:].rearrange("p (t j) -> p t j", j=PAIRS),
+                        func=ACT.Sin,
+                        scale=scale,
+                        bias=bias,
+                    )
 
             nothing = (0, 0, 0)
             turn(x_raw[0], 2, x_codes, x_scales, 0, False, nothing)
@@ -349,7 +349,7 @@ def tile_mpselfattentiontorch_pa_kernel(
                 )
             nc.scalar.activation(out=rstd[:, 0:tiles], in_=mean[:, 0:tiles], func=ACT.Abs_reciprocal_sqrt)
             for t in range(tiles):
-                scaled_trig[(n, t)] = small.tile([P, 2 * P], F32, name="scaled_trig", tag="scaled_trig", bufs=8)
+                scaled_trig[(n, t)] = small.tile([P, 3 * PAIRS], F32, name="scaled_trig", tag="scaled_trig", bufs=8)
                 nc.scalar.activation(
                     out=scaled_trig[(n, t)][:], in_=trig[:, tile0 + t, :], func=ACT.Copy, scale=rstd[:, t : t + 1]
                 )
@@ -393,16 +393,16 @@ def tile_mpselfattentiontorch_pa_kernel(
                 straight = rope_pool.tile([P, 4 * P], F32, name="straight", tag="straight")
                 crossed = rope_pool.tile([P, 4 * P], F32, name="crossed", tag="crossed")
                 nc.vector.tensor_tensor(
-                    out=straight[:].rearrange("p (h c) -> p h c", h=BANK_HEADS),
-                    in0=back[:].rearrange("p (h c) -> p h c", h=BANK_HEADS),
-                    in1=factors[:, 0:P].unsqueeze(1).to_broadcast([P, BANK_HEADS, P]),
+                    out=straight[:].rearrange("p (h j r) -> p h j r", h=BANK_HEADS, r=2),
+                    in0=back[:].rearrange("p (h j r) -> p h j r", h=BANK_HEADS, r=2),
+                    in1=factors[:, 0:PAIRS].unsqueeze(1).unsqueeze(3).to_broadcast([P, BANK_HEADS, PAIRS, 2]),
                     op=ALU.mult,
                 )
                 nc.vector.tensor_tensor(
                     out=crossed[:].rearrange("p (h j r) -> p h j r", h=BANK_HEADS, r=2),
                     in0=back[:].rearrange("p (h j r) -> p h j r", h=BANK_HEADS, r=2)[:, :, :, ::-1],
-                    in1=factors[:, P : 2 * P]
-                    .rearrange("p (j r) -> p j r", r=2)
+                    in1=factors[:, PAIRS : 3 * PAIRS]
+                    .rearrange("p (r j) -> p j r", r=2)
                     .unsqueeze(1)
                     .to_broadcast([P, BANK_HEADS, PAIRS, 2]),
                     op=ALU.mult,

@@ -38,7 +38,7 @@ STEP_HEADS = 3
 STEPS = HEADS // STEP_HEADS
 BANK_HEADS = 4
 BANKS = HEADS // BANK_HEADS
-ROPE_BANKS = (2, 2, 3, 2)
+ROPE_BANKS = (0, 3, 3, 3)
 ROW_PAIRS = CH // (2 * P)
 HALF = K // 2
 WIDEN_BESIDE = (1, 1, 0)
@@ -56,12 +56,12 @@ def tile_mpselfattentiontorch_pa_kernel(
         ctx.enter_context(tc.manual_schedule(engines={mybir.EngineType.PE, mybir.EngineType.DVE}))
         const = ctx.enter_context(tc.tile_pool(name="const", bufs=1))
         bytes_pool = ctx.enter_context(tc.tile_pool(name="bytes", bufs=2))
-        wide_pool = ctx.enter_context(tc.tile_pool(name="wide", bufs=ROW_PAIRS))
+        wide_pool = ctx.enter_context(tc.tile_pool(name="wide", bufs=ROW_PAIRS - 1))
         grouped_pool = ctx.enter_context(tc.tile_pool(name="grouped", bufs=3))
         heads_pool = ctx.enter_context(tc.tile_pool(name="heads", bufs=1))
         mx_psum = ctx.enter_context(tc.psum_pool(name="mx_psum", bufs=3))
-        back_psum = ctx.enter_context(tc.psum_pool(name="back_psum", bufs=3))
-        turn_psum = ctx.enter_context(tc.psum_pool(name="turn_psum", bufs=2))
+        back_psum = ctx.enter_context(tc.psum_pool(name="t_psum", bufs=5))
+        turn_psum = back_psum
 
         ident_f32 = const.tile([P, P], F32, name="ident_f32")
         ident_bf16 = const.tile([P, P], BF16, name="ident_bf16")
@@ -90,7 +90,7 @@ def tile_mpselfattentiontorch_pa_kernel(
             if first_unit[0] and turned[0] % 5 >= 2:
                 bank = back_psum.tile([P, 4 * P], F32, name="turn_bank2", tag="back")
             else:
-                bank = turn_psum.tile([P, 4 * P], F32, name="turn_bank", tag="turn")
+                bank = turn_psum.tile([P, 4 * P], F32, name="turn_bank", tag="back")
             for t in range(tiles):
                 words = rows[:, t, :].bitcast(F32)
                 for u in range(2):
@@ -176,7 +176,7 @@ def tile_mpselfattentiontorch_pa_kernel(
             c = proj * HEADS + h
             gained[(n, h)] = heads_pool.tile([P, UNIT_WIDTH], F32, name="gained", tag="gained", bufs=2 * HEADS)
             squared[(n, h)] = heads_pool.tile(
-                [P, UNIT_WIDTH], F32, name="squared", tag="squared", bufs=HEADS + STEP_HEADS + 1
+                [P, UNIT_WIDTH], F32, name="squared", tag="squared", bufs=2 * HEADS
             )
             nc.scalar.activation(
                 out=gained[(n, h)][:, 0:width],
@@ -249,7 +249,7 @@ def tile_mpselfattentiontorch_pa_kernel(
                 shifted = setup.tile([P, TOKEN_TILES * PAIRS], F32, name="shifted")
                 folded = setup.tile([P, TOKEN_TILES * PAIRS], F32, name="folded")
                 for lo, hi in ((0, 8), (8, TOKEN_TILES)):
-                    angles = turn_psum.tile([P, 4 * P], F32, name="angles", tag="turn")
+                    angles = turn_psum.tile([P, 4 * P], F32, name="angles", tag="back")
                     for tile in range(lo, hi):
                         nc.tensor.matmul(
                             out=angles[:, (tile - lo) * PAIRS : (tile - lo + 1) * PAIRS],
@@ -286,7 +286,7 @@ def tile_mpselfattentiontorch_pa_kernel(
             turn(wk_raw[0], 2, w_codes[KEY], w_scales[KEY], 0, True, nothing)
             wk_raw[4] = load_rows(wk, 8 * P, 2)
 
-            columns = turn_psum.tile([P, P], BF16, name="columns", tag="turn")
+            columns = turn_psum.tile([P, P], BF16, name="columns", tag="back")
             nc.tensor.transpose(columns[:], vectors[:], ident_bf16[:])
             nc.vector.tensor_copy(out=per_channel[:], in_=columns[:, 0 : 4 * HEADS])
             nc.vector.tensor_tensor(
@@ -322,37 +322,28 @@ def tile_mpselfattentiontorch_pa_kernel(
 
         scaled_trig = {}
 
-        def norm(n):
-            tile0, tiles = UNITS[n][1], UNITS[n][2]
-            sums = turn_psum.tile([P, 4 * P], F32, name="sums", tag="turn")
-            for t in range(tiles):
-                for h in range(HEADS):
-                    nc.tensor.matmul(
-                        out=sums[:, t * P : (t + 1) * P],
-                        lhsT=squared[(n, h)][:, t * P : (t + 1) * P],
-                        rhs=ident_f32[:],
-                        is_transpose=True,
-                        start=(h == 0),
-                        stop=(h == HEADS - 1),
-                    )
-            mean = small.tile([P, 4], F32, name="mean", tag="mean")
-            rstd = small.tile([P, 4], F32, name="rstd", tag="rstd")
-            for t in range(tiles):
-                unused = small.tile([P, P], F32, name="unused", tag="unused")
-                nc.scalar.activation(
-                    out=unused[:],
-                    in_=sums[:, t * P : (t + 1) * P],
-                    func=ACT.Identity,
-                    scale=1.0 / CH,
-                    bias=EPS / P,
-                    accum_out=mean[:, t : t + 1],
+        def norm(n, t):
+            tile0 = UNITS[n][1]
+            sums = turn_psum.tile([P, 4 * P], F32, name="sums", tag="back")
+            for h in range(HEADS):
+                nc.tensor.matmul(
+                    out=sums[:, 0:P],
+                    lhsT=squared[(n, h)][:, t * P : (t + 1) * P],
+                    rhs=ident_f32[:],
+                    is_transpose=True,
+                    start=(h == 0),
+                    stop=(h == HEADS - 1),
                 )
-            nc.scalar.activation(out=rstd[:, 0:tiles], in_=mean[:, 0:tiles], func=ACT.Abs_reciprocal_sqrt)
-            for t in range(tiles):
-                scaled_trig[(n, t)] = small.tile([P, 3 * PAIRS], F32, name="scaled_trig", tag="scaled_trig", bufs=8)
-                nc.scalar.activation(
-                    out=scaled_trig[(n, t)][:], in_=trig[:, tile0 + t, :], func=ACT.Copy, scale=rstd[:, t : t + 1]
-                )
+            mean = small.tile([P, 1], F32, name="mean", tag="mean")
+            rstd = small.tile([P, 1], F32, name="rstd", tag="rstd")
+            unused = small.tile([P, P], F32, name="unused", tag="unused")
+            nc.scalar.activation(
+                out=unused[:], in_=sums[:, 0:P], func=ACT.Identity, scale=1.0 / CH, bias=EPS / P, accum_out=mean[:]
+            )
+            nc.scalar.activation(out=rstd[:], in_=mean[:], func=ACT.Abs_reciprocal_sqrt)
+            scaled_trig[(n, t)] = small.tile([P, 3 * PAIRS], F32, name="scaled_trig", tag="scaled_trig", bufs=8)
+            nc.scalar.activation(out=scaled_trig[(n, t)][:], in_=trig[:, tile0 + t, :], func=ACT.Copy, scale=rstd[:])
+            normed[0] += BANKS
 
         banks = []
         for n in range(len(UNITS)):
@@ -421,9 +412,8 @@ def tile_mpselfattentiontorch_pa_kernel(
                 for h in range(STEP_HEADS * s, STEP_HEADS * (s + 1)):
                     project(n, h)
                 rotate(ROPE_BANKS[s])
-                if s == 0:
-                    norm(n - 1)
-                    normed[0] += BANKS * UNITS[n - 1][2]
+                if s < UNITS[n - 1][2]:
+                    norm(n - 1, s)
                 step += 1
                 due = min(wq_banks, (wq_banks * step + wq_steps - 1) // wq_steps)
                 for i in range(wq_turned, due):
@@ -433,7 +423,6 @@ def tile_mpselfattentiontorch_pa_kernel(
                     widen(1)
                 wq_turned = due
         rotate(len(banks))
-        norm(len(UNITS) - 1)
-        normed[0] = len(banks)
+        norm(len(UNITS) - 1, 0)
         rotate(len(banks))
         add_and_store()

@@ -193,12 +193,14 @@ def tile_mpselfattentiontorch_pa_kernel(
             rows_pool = early.enter_context(tc.tile_pool(name="rows", bufs=4))
             setup = early.enter_context(tc.tile_pool(name="setup", bufs=1))
 
-            def load_rows(dram, row0, tiles):
+            def load_rows(dram, row0, tiles, pieces=1):
                 rows = rows_pool.tile([P, 2, K], BF16, name="rows", tag="rows")
-                nc.sync.dma_start(
-                    out=rows[:, 0:tiles, :],
-                    in_=dram[row0 : row0 + tiles * P, :].rearrange("(t p) k -> p t k", p=P),
-                )
+                for c in range(pieces):
+                    cols = slice(c * K // pieces, (c + 1) * K // pieces)
+                    nc.sync.dma_start(
+                        out=rows[:, 0:tiles, cols],
+                        in_=dram[row0 : row0 + tiles * P, cols].rearrange("(t p) k -> p t k", p=P),
+                    )
                 return rows
 
             nc.vector.memset(vectors[:], 0.0)
@@ -216,7 +218,7 @@ def tile_mpselfattentiontorch_pa_kernel(
                 out=angle_rows[ROW_W : ROW_W + WIDTH, BY_FRAME + BY_HEIGHT : PAIRS],
                 in_=theta[0:WIDTH, BY_FRAME + BY_HEIGHT : PAIRS],
             )
-            x_raw = {0: load_rows(x_rows, 0, 2), 1: load_rows(x_rows, 2 * P, 2)}
+            x_raw = {0: load_rows(x_rows, 0, 2, PASSES), 1: load_rows(x_rows, 2 * P, 2, 1)}
             wk_raw = {0: load_rows(wk, 0, 2), 1: load_rows(wk, 2 * P, 2)}
             nc.sync.dma_start(out=scale_rows[:], in_=wq_scale.rearrange("o k -> (o k)").partition_broadcast(P))
             load_bytes(0)
@@ -404,8 +406,9 @@ def tile_mpselfattentiontorch_pa_kernel(
                 rotated[0] += 1
 
         wq_banks = PASSES * ROW_PAIRS
-        wq_steps = 2 * STEPS
+        wq_steps = 10
         wq_turned = 0
+        pending = []
         step = 0
         for n in range(1, len(UNITS)):
             for s in range(STEPS):
@@ -419,9 +422,14 @@ def tile_mpselfattentiontorch_pa_kernel(
                 for i in range(wq_turned, due):
                     j, g = i // PASSES, i % PASSES
                     widen(max(0, 4 * (j + 1) - widened[0]))
-                    quantise(turn_bank(wq_wide[j], 2, g, w_codes[Q], w_scales[Q], 2 * P * j, False))
+                    pending.append(turn_bank(wq_wide[j], 2, g, w_codes[Q], w_scales[Q], 2 * P * j, False))
                     widen(1)
+                    if len(pending) > 1:
+                        quantise(pending.pop(0))
                 wq_turned = due
+                if due == wq_banks:
+                    while pending:
+                        quantise(pending.pop(0))
         rotate(len(banks))
         norm(len(UNITS) - 1, 0)
         rotate(len(banks))

@@ -203,6 +203,9 @@ def tile_mpselfattentiontorch_pa_kernel(
                     )
                 return rows
 
+            warm = setup.tile([P, 2], F32, name="warm")
+            nc.vector.memset(warm[:], 0.0)
+            nc.scalar.activation(out=warm[:, 1:2], in_=warm[:, 0:1], func=ACT.Sin)
             nc.vector.memset(vectors[:], 0.0)
             nc.vector.memset(angle_rows[:], 0.0)
             for i, v in enumerate((bq, bk, gq, gk)):
@@ -313,7 +316,7 @@ def tile_mpselfattentiontorch_pa_kernel(
                     x_raw[4] = load_rows(x_rows, 8 * P, 1)
                 project(0, 2 * pair)
                 project(0, 2 * pair + 1)
-                if pair == 1:
+                if pair == 0:
                     make_trig()
             turn(x_raw[3], 2, x_codes, x_scales, 6 * P, True, WIDEN_BESIDE)
             turn(x_raw[4], 1, x_codes, x_scales, 8 * P, True, WIDEN_BESIDE)

@@ -34,11 +34,11 @@ Q, KEY = 0, 1
 UNITS = ((KEY, 0, 3), (KEY, 3, 3), (KEY, 6, 3), (Q, 0, 3), (Q, 3, 3), (Q, 6, 2), (Q, 8, 1))
 UNIT_WIDTH = 3 * P
 COLUMN_GROUPS = {3: ((0, 256), (256, 128)), 2: ((0, 256),), 1: ((0, 128),)}
-STEP_HEADS = 3
+STEP_HEADS = 2
 STEPS = HEADS // STEP_HEADS
 BANK_HEADS = 4
 BANKS = HEADS // BANK_HEADS
-ROPE_BANKS = (0, 3, 3, 3)
+ROPE_BANKS = (0, 3, 0, 3, 0, 3)
 ROW_PAIRS = CH // (2 * P)
 HALF = K // 2
 WIDEN_BESIDE = (1, 1, 0)
@@ -409,7 +409,7 @@ def tile_mpselfattentiontorch_pa_kernel(
                 rotated[0] += 1
 
         wq_banks = PASSES * ROW_PAIRS
-        wq_steps = 10
+        wq_steps = 15
         wq_turned = 0
         pending = []
         step = 0
@@ -418,8 +418,8 @@ def tile_mpselfattentiontorch_pa_kernel(
                 for h in range(STEP_HEADS * s, STEP_HEADS * (s + 1)):
                     project(n, h)
                 rotate(ROPE_BANKS[s])
-                if s < UNITS[n - 1][2]:
-                    norm(n - 1, s)
+                if s % 2 == 0 and s // 2 < UNITS[n - 1][2]:
+                    norm(n - 1, s // 2)
                 step += 1
                 due = min(wq_banks, (wq_banks * step + wq_steps - 1) // wq_steps)
                 for i in range(wq_turned, due):

@@ -228,27 +228,23 @@ def tile_mpselfattentiontorch_pa_kernel(
             load_bytes(1)
             make_identity(nc, ident_f32[:])
 
-            diff_f = setup.tile([P, TOKENS], I32, name="diff_f", tag="scratch", bufs=2)
-            diff_h = setup.tile([P, TOKENS], I32, name="diff_h", tag="scratch", bufs=2)
-            nc.gpsimd.iota(diff_f[:], pattern=[[1, FRAMES], [0, HEIGHT * WIDTH]], base=0, channel_multiplier=-1)
-            nc.gpsimd.iota(
-                diff_h[:], pattern=[[0, FRAMES], [1, HEIGHT], [0, WIDTH]], base=ROW_H, channel_multiplier=-1
-            )
-            make_identity(nc, ident_bf16[:])
-            picks_f = setup.tile([P, TOKENS], BF16, name="picks_f")
-            picks_fh = setup.tile([P, TOKENS], BF16, name="picks_fh")
             picks = setup.tile([P, TOKENS], BF16, name="picks")
-            nc.vector.tensor_scalar(out=picks_f[:], in0=diff_f[:], scalar1=0.0, scalar2=None, op0=ALU.is_equal)
-            diff_w = setup.tile([P, TOKENS], I32, name="diff_w", tag="scratch", bufs=2)
-            nc.gpsimd.iota(
-                diff_w[:], pattern=[[0, FRAMES * HEIGHT], [1, WIDTH]], base=ROW_W, channel_multiplier=-1
-            )
-            nc.vector.scalar_tensor_tensor(
-                out=picks_fh[:], in0=diff_h[:], scalar=0.0, in1=picks_f[:], op0=ALU.is_equal, op1=ALU.add
-            )
-            nc.vector.scalar_tensor_tensor(
-                out=picks[:], in0=diff_w[:], scalar=0.0, in1=picks_fh[:], op0=ALU.is_equal, op1=ALU.add
-            )
+            nc.vector.memset(picks[:], 0.0)
+            for pattern, first_row in (
+                ([[1, FRAMES], [0, HEIGHT * WIDTH]], 0),
+                ([[0, FRAMES], [1, HEIGHT], [0, WIDTH]], ROW_H),
+                ([[0, FRAMES * HEIGHT], [1, WIDTH]], ROW_W),
+            ):
+                nc.gpsimd.affine_select(
+                    out=picks[:],
+                    in_=picks[:],
+                    pattern=pattern,
+                    compare_op=ALU.not_equal,
+                    fill=1.0,
+                    base=first_row,
+                    channel_multiplier=-1,
+                )
+            make_identity(nc, ident_bf16[:])
 
             def make_trig():
                 shifted = setup.tile([P, TOKEN_TILES * PAIRS], F32, name="shifted")

@@ -101,7 +101,7 @@ def tile_mpselfattentiontorch_pa_kernel(
             grouped = grouped_pool.tile([P, 8 * P], BF16, name="grouped", tag="grouped", align_bytes=64)
             dst = grouped[:, 0 : 4 * n].bitcast(F32).rearrange("p (t r u) -> p t r u", t=tiles, u=2)
             src = bank[:, 0 : 2 * n].rearrange("p (t u r) -> p t r u", t=tiles, u=2)
-            if share and turned[0] % 2 == 1:
+            if share and turned[0] % 4 == 1:
                 nc.vector.tensor_copy(out=dst, in_=src)
             else:
                 nc.scalar.copy(out=dst, in_=src)

@@ -71,15 +71,15 @@ def tile_mpselfattentiontorch_pa_kernel(
         angle_rows = const.tile([P, PAIRS], BF16, name="angle_rows")
         trig = const.tile([P, TOKEN_TILES, 3 * PAIRS], F32, name="trig")
         scale_rows = const.tile([P, K], F32, name="scale_rows")
-        x_codes = const.tile([P, PASSES, TOKENS], U32, name="x_codes", align_bytes=64)
-        x_scales = const.tile([P, PASSES, TOKENS], U8, name="x_scales", align_bytes=64)
+        x_codes = const.tile([P, PASSES, TOKENS], U32, name="x_codes", align_bytes=256)
+        x_scales = const.tile([P, PASSES, TOKENS], U8, name="x_scales", align_bytes=256)
         w_codes = (
-            const.tile([P, PASSES, CH], U32, name="wq_codes", align_bytes=64),
-            const.tile([P, PASSES, CH], U32, name="wk_codes", align_bytes=64),
+            const.tile([P, PASSES, CH], U32, name="wq_codes", align_bytes=256),
+            const.tile([P, PASSES, CH], U32, name="wk_codes", align_bytes=256),
         )
         w_scales = (
-            const.tile([P, PASSES, CH], U8, name="wq_scales", align_bytes=64),
-            const.tile([P, PASSES, CH], U8, name="wk_scales", align_bytes=64),
+            const.tile([P, PASSES, CH], U8, name="wq_scales", align_bytes=256),
+            const.tile([P, PASSES, CH], U8, name="wk_scales", align_bytes=256),
         )
 
         turned = [0]

@@ -63,7 +63,7 @@ def tile_mpselfattentiontorch_pa_kernel(
         back_psum = ctx.enter_context(tc.psum_pool(name="t_psum", bufs=5))
         turn_psum = back_psum
 
-        ident_f32 = const.tile([P, P], F32, name="ident_f32")
+        ident_f32 = const.tile([P, P], F32, name="ident_f32", align_bytes=256)
         ident_bf16 = const.tile([P, P], BF16, name="ident_bf16")
         vectors = const.tile([P, P], BF16, name="vectors")
         per_channel = const.tile([P, 4 * HEADS], F32, name="per_channel")
@@ -131,7 +131,7 @@ def tile_mpselfattentiontorch_pa_kernel(
             for i in range(widened[0], upto):
                 j, t, half = i // 4, (i // 2) % 2, i % 2
                 if i % 4 == 0:
-                    wq_wide[j] = wide_pool.tile([P, 2, K], BF16, name="wq_wide", tag="wq_wide")
+                    wq_wide[j] = wide_pool.tile([P, 2, K], BF16, name="wq_wide", tag="wq_wide", align_bytes=256)
                 cols = slice(half * HALF, (half + 1) * HALF)
                 nc.vector.tensor_tensor(
                     out=wq_wide[j][:, t, cols],
@@ -174,9 +174,11 @@ def tile_mpselfattentiontorch_pa_kernel(
                         stop=(g == PASSES - 1),
                     )
             c = proj * HEADS + h
-            gained[(n, h)] = heads_pool.tile([P, UNIT_WIDTH], F32, name="gained", tag="gained", bufs=2 * HEADS)
+            gained[(n, h)] = heads_pool.tile(
+                [P, UNIT_WIDTH], F32, name="gained", tag="gained", bufs=2 * HEADS, align_bytes=256
+            )
             squared[(n, h)] = heads_pool.tile(
-                [P, UNIT_WIDTH], F32, name="squared", tag="squared", bufs=2 * HEADS
+                [P, UNIT_WIDTH], F32, name="squared", tag="squared", bufs=2 * HEADS, align_bytes=256
             )
             nc.scalar.activation(
                 out=gained[(n, h)][:, 0:width],
@@ -194,7 +196,7 @@ def tile_mpselfattentiontorch_pa_kernel(
             setup = early.enter_context(tc.tile_pool(name="setup", bufs=1))
 
             def load_rows(dram, row0, tiles, pieces=1):
-                rows = rows_pool.tile([P, 2, K], BF16, name="rows", tag="rows")
+                rows = rows_pool.tile([P, 2, K], BF16, name="rows", tag="rows", align_bytes=256)
                 for c in range(pieces):
                     cols = slice(c * K // pieces, (c + 1) * K // pieces)
                     nc.sync.dma_start(

@@ -42,7 +42,7 @@ ROPE_BANKS = (0, 3, 0, 3, 0, 3)
 ROW_PAIRS = CH // (2 * P)
 HALF = K // 2
 WIDEN_BESIDE = (1, 1, 0)
-VECTOR_ADDS = 3
+VECTOR_ADDS = 5
 
 
 def tile_mpselfattentiontorch_pa_kernel(
@@ -69,8 +69,8 @@ def tile_mpselfattentiontorch_pa_kernel(
         per_channel = const.tile([P, 4 * HEADS], F32, name="per_channel")
         bias_gain = const.tile([P, 2 * HEADS], F32, name="bias_gain")
         angle_rows = const.tile([P, PAIRS], BF16, name="angle_rows")
-        trig = const.tile([P, TOKEN_TILES, 3 * PAIRS], F32, name="trig")
-        scale_rows = const.tile([P, K], F32, name="scale_rows")
+        trig = const.tile([P, TOKEN_TILES, 3 * PAIRS], F32, name="trig", align_bytes=256)
+        scale_rows = const.tile([P, K], F32, name="scale_rows", align_bytes=256)
         x_codes = const.tile([P, PASSES, TOKENS], U32, name="x_codes", align_bytes=256)
         x_scales = const.tile([P, PASSES, TOKENS], U8, name="x_scales", align_bytes=256)
         w_codes = (
@@ -98,7 +98,7 @@ def tile_mpselfattentiontorch_pa_kernel(
                     nc.tensor.transpose(
                         bank[:, c : c + P], words[:, WORDS * g + u : WORDS * (g + 1) : 2], ident_f32[:]
                     )
-            grouped = grouped_pool.tile([P, 8 * P], BF16, name="grouped", tag="grouped", align_bytes=64)
+            grouped = grouped_pool.tile([P, 8 * P], BF16, name="grouped", tag="grouped", align_bytes=256)
             dst = grouped[:, 0 : 4 * n].bitcast(F32).rearrange("p (t r u) -> p t r u", t=tiles, u=2)
             src = bank[:, 0 : 2 * n].rearrange("p (t u r) -> p t r u", t=tiles, u=2)
             if share and turned[0] % 4 == 1:
@@ -121,7 +121,7 @@ def tile_mpselfattentiontorch_pa_kernel(
         widened = [0]
 
         def load_bytes(j):
-            wq_raw[j] = bytes_pool.tile([P, 2, K], U8, name="wq_raw", tag="wq_raw")
+            wq_raw[j] = bytes_pool.tile([P, 2, K], U8, name="wq_raw", tag="wq_raw", align_bytes=256)
             nc.sync.dma_start(
                 out=wq_raw[j][:], in_=wq_bytes[2 * P * j : 2 * P * (j + 1), :].rearrange("(t p) k -> p t k", p=P)
             )
@@ -344,7 +344,9 @@ def tile_mpselfattentiontorch_pa_kernel(
                 out=unused[:], in_=sums[:, 0:P], func=ACT.Identity, scale=1.0 / CH, bias=EPS / P, accum_out=mean[:]
             )
             nc.scalar.activation(out=rstd[:], in_=mean[:], func=ACT.Abs_reciprocal_sqrt)
-            scaled_trig[(n, t)] = small.tile([P, 3 * PAIRS], F32, name="scaled_trig", tag="scaled_trig", bufs=8)
+            scaled_trig[(n, t)] = small.tile(
+                [P, 3 * PAIRS], F32, name="scaled_trig", tag="scaled_trig", bufs=8, align_bytes=256
+            )
             nc.scalar.activation(out=scaled_trig[(n, t)][:], in_=trig[:, tile0 + t, :], func=ACT.Copy, scale=rstd[:])
             normed[0] += BANKS
 
@@ -360,7 +362,7 @@ def tile_mpselfattentiontorch_pa_kernel(
 
         def add_and_store():
             proj, tile, b, straight, crossed = products.pop(0)
-            result = rope_pool.tile([P, 4 * P], F32, name="result", tag="result", bufs=6)
+            result = rope_pool.tile([P, 4 * P], F32, name="result", tag="result", bufs=6, align_bytes=256)
             if added[0] >= len(banks) - VECTOR_ADDS and added[0] % 2 == 1:
                 nc.vector.tensor_tensor(out=result[:], in0=straight[:], in1=crossed[:], op=ALU.add)
             else:
@@ -384,8 +386,8 @@ def tile_mpselfattentiontorch_pa_kernel(
                         ident_f32[:],
                     )
                 factors = scaled_trig[(n, t)]
-                straight = rope_pool.tile([P, 4 * P], F32, name="straight", tag="straight")
-                crossed = rope_pool.tile([P, 4 * P], F32, name="crossed", tag="crossed")
+                straight = rope_pool.tile([P, 4 * P], F32, name="straight", tag="straight", align_bytes=256)
+                crossed = rope_pool.tile([P, 4 * P], F32, name="crossed", tag="crossed", align_bytes=256)
                 nc.vector.tensor_tensor(
                     out=straight[:].rearrange("p (h j r) -> p h j r", h=BANK_HEADS, r=2),
                     in0=back[:].rearrange("p (h j r) -> p h j r", h=BANK_HEADS, r=2),

from contextlib import ExitStack
import math

import concourse.mybir as mybir
from concourse.masks import make_identity

F32 = mybir.dt.float32
BF16 = mybir.dt.bfloat16
U32 = mybir.dt.uint32
U8 = mybir.dt.uint8
I32 = mybir.dt.int32
FP8 = mybir.dt.float8_e4m3fn
FP8X4 = mybir.dt.float8_e4m3fn_x4
ALU = mybir.AluOpType
ACT = mybir.ActivationFunctionType

P = 128
TOKENS = 1152
TOKEN_TILES = TOKENS // P
K = 1536
CH = 1536
HEADS = CH // P
PASSES = K // (4 * P)
WORDS = 2 * P
FRAMES, HEIGHT, WIDTH = 6, 8, 24
PAIRS = 64
BY_FRAME, BY_HEIGHT = 22, 21
ROW_H, ROW_W = FRAMES, FRAMES + HEIGHT
EPS = 1e-6
PI_BELOW = 3.1415925
FLOPS = 2 * TOKENS * K * 2 * CH

Q, KEY = 0, 1
UNITS = ((KEY, 0, 3), (KEY, 3, 3), (KEY, 6, 3), (Q, 0, 3), (Q, 3, 3), (Q, 6, 2), (Q, 8, 1))
UNIT_WIDTH = 3 * P
COLUMN_GROUPS = {3: ((0, 256), (256, 128)), 2: ((0, 256),), 1: ((0, 128),)}
STEP_HEADS = 2
STEPS = HEADS // STEP_HEADS
BANK_HEADS = 4
BANKS = HEADS // BANK_HEADS
ROPE_BANKS = (0, 3, 0, 3, 0, 3)
ROW_PAIRS = CH // (2 * P)
HALF = K // 2
WIDEN_BESIDE = (1, 1, 0)
VECTOR_ADDS = 5


def tile_mpselfattentiontorch_pa_kernel(
    tc, x, theta, wq_bytes, wq_scale, bq, wk, bk, gq, gk, out_0, out_1
):
    nc = tc.nc
    outs = (out_0, out_1)
    x_rows = x.flatten_outer_dims()

    with ExitStack() as ctx:
        ctx.enter_context(tc.manual_schedule(engines={mybir.EngineType.PE, mybir.EngineType.DVE}))
        const = ctx.enter_context(tc.tile_pool(name="const", bufs=1))
        bytes_pool = ctx.enter_context(tc.tile_pool(name="bytes", bufs=2))
        wide_pool = ctx.enter_context(tc.tile_pool(name="wide", bufs=ROW_PAIRS - 1))
        grouped_pool = ctx.enter_context(tc.tile_pool(name="grouped", bufs=3))
        heads_pool = ctx.enter_context(tc.tile_pool(name="heads", bufs=1))
        mx_psum = ctx.enter_context(tc.psum_pool(name="mx_psum", bufs=3))
        back_psum = ctx.enter_context(tc.psum_pool(name="t_psum", bufs=5))
        turn_psum = back_psum

        ident_f32 = const.tile([P, P], F32, name="ident_f32", align_bytes=256)
        ident_bf16 = const.tile([P, P], BF16, name="ident_bf16")
        vectors = const.tile([P, P], BF16, name="vectors")
        per_channel = const.tile([P, 4 * HEADS], F32, name="per_channel")
        bias_gain = const.tile([P, 2 * HEADS], F32, name="bias_gain")
        angle_rows = const.tile([P, PAIRS], BF16, name="angle_rows")
        trig = const.tile([P, TOKEN_TILES, 3 * PAIRS], F32, name="trig", align_bytes=256)
        scale_rows = const.tile([P, K], F32, name="scale_rows", align_bytes=256)
        x_codes = const.tile([P, PASSES, TOKENS], U32, name="x_codes", align_bytes=256)
        x_scales = const.tile([P, PASSES, TOKENS], U8, name="x_scales", align_bytes=256)
        w_codes = (
            const.tile([P, PASSES, CH], U32, name="wq_codes", align_bytes=256),
            const.tile([P, PASSES, CH], U32, name="wk_codes", align_bytes=256),
        )
        w_scales = (
            const.tile([P, PASSES, CH], U8, name="wq_scales", align_bytes=256),
            const.tile([P, PASSES, CH], U8, name="wk_scales", align_bytes=256),
        )

        turned = [0]
        first_unit = [True]

        def turn_bank(rows, tiles, g, codes, scales, col0, share):
            n = tiles * P
            if first_unit[0] and turned[0] % 5 >= 2:
                bank = back_psum.tile([P, 4 * P], F32, name="turn_bank2", tag="back")
            else:
                bank = turn_psum.tile([P, 4 * P], F32, name="turn_bank", tag="back")
            for t in range(tiles):
                words = rows[:, t, :].bitcast(F32)
                for u in range(2):
                    c = (2 * t + u) * P
                    nc.tensor.transpose(
                        bank[:, c : c + P], words[:, WORDS * g + u : WORDS * (g + 1) : 2], ident_f32[:]
                    )
            grouped = grouped_pool.tile([P, 8 * P], BF16, name="grouped", tag="grouped", align_bytes=256)
            dst = grouped[:, 0 : 4 * n].bitcast(F32).rearrange("p (t r u) -> p t r u", t=tiles, u=2)
            src = bank[:, 0 : 2 * n].rearrange("p (t u r) -> p t r u", t=tiles, u=2)
            if share and turned[0] % 4 == 1:
                nc.vector.tensor_copy(out=dst, in_=src)
            else:
                nc.scalar.copy(out=dst, in_=src)
            turned[0] += 1
            return (codes, scales, g, col0, n, grouped)

        def quantise(job):
            codes, scales, g, col0, n, grouped = job
            nc.vector.quantize_mx(
                out=codes[:, g, col0 : col0 + n].bitcast(FP8X4),
                scales=scales[:, g, col0 : col0 + n],
                in_=grouped[:, 0 : 4 * n],
            )

        wq_raw = {}
        wq_wide = {}
        widened = [0]

        def load_bytes(j):
            wq_raw[j] = bytes_pool.tile([P, 2, K], U8, name="wq_raw", tag="wq_raw", align_bytes=256)
            nc.sync.dma_start(
                out=wq_raw[j][:], in_=wq_bytes[2 * P * j : 2 * P * (j + 1), :].rearrange("(t p) k -> p t k", p=P)
            )

        def widen(count):
            upto = min(widened[0] + count, 4 * ROW_PAIRS)
            for i in range(widened[0], upto):
                j, t, half = i // 4, (i // 2) % 2, i % 2
                if i % 4 == 0:
                    wq_wide[j] = wide_pool.tile([P, 2, K], BF16, name="wq_wide", tag="wq_wide", align_bytes=256)
                cols = slice(half * HALF, (half + 1) * HALF)
                nc.vector.tensor_tensor(
                    out=wq_wide[j][:, t, cols],
                    in0=wq_raw[j][:, t, cols].bitcast(FP8),
                    in1=scale_rows[:, cols],
                    op=ALU.mult,
                )
                if i % 4 == 3 and j + 2 < ROW_PAIRS:
                    load_bytes(j + 2)
            widened[0] = upto

        def turn(rows, tiles, codes, scales, col0, share, beside):
            waiting = None
            for g in range(PASSES):
                job = turn_bank(rows, tiles, g, codes, scales, col0, share)
                if waiting is not None:
                    quantise(waiting)
                waiting = job
                widen(beside[g])
            quantise(waiting)

        gained = {}
        squared = {}

        def project(n, h):
            proj, tile0, tiles = UNITS[n]
            width = tiles * P
            acc = mx_psum.tile([P, 4 * P], F32, name="acc", tag="acc")
            chans = slice(h * P, (h + 1) * P)
            for c0, cols in COLUMN_GROUPS[tiles]:
                toks = slice(tile0 * P + c0, tile0 * P + c0 + cols)
                for g in range(PASSES):
                    nc.tensor.matmul_mx(
                        out=acc[:, c0 : c0 + cols],
                        lhsT=w_codes[proj][:, g, chans].bitcast(FP8X4),
                        lhsT_scale=w_scales[proj][:, g, chans],
                        rhs=x_codes[:, g, toks].bitcast(FP8X4),
                        rhs_scale=x_scales[:, g, toks],
                        start=(g == 0),
                        stop=(g == PASSES - 1),
                    )
            c = proj * HEADS + h
            gained[(n, h)] = heads_pool.tile(
                [P, UNIT_WIDTH], F32, name="gained", tag="gained", bufs=2 * HEADS, align_bytes=256
            )
            squared[(n, h)] = heads_pool.tile(
                [P, UNIT_WIDTH], F32, name="squared", tag="squared", bufs=2 * HEADS, align_bytes=256
            )
            nc.scalar.activation(
                out=gained[(n, h)][:, 0:width],
                in_=acc[:, 0:width],
                func=ACT.Identity,
                bias=bias_gain[:, c : c + 1],
                scale=per_channel[:, 2 * HEADS + c : 2 * HEADS + c + 1],
            )
            nc.scalar.activation(
                out=squared[(n, h)][:, 0:width], in_=acc[:, 0:width], func=ACT.Square, bias=per_channel[:, c : c + 1]
            )

        with ExitStack() as early:
            rows_pool = early.enter_context(tc.tile_pool(name="rows", bufs=4))
            setup = early.enter_context(tc.tile_pool(name="setup", bufs=1))

            def load_rows(dram, row0, tiles, pieces=1):
                rows = rows_pool.tile([P, 2, K], BF16, name="rows", tag="rows", align_bytes=256)
                for c in range(pieces):
                    cols = slice(c * K // pieces, (c + 1) * K // pieces)
                    nc.sync.dma_start(
                        out=rows[:, 0:tiles, cols],
                        in_=dram[row0 : row0 + tiles * P, cols].rearrange("(t p) k -> p t k", p=P),
                    )
                return rows

            warm = setup.tile([P, 2], F32, name="warm")
            nc.vector.memset(warm[:], 0.0)
            nc.scalar.activation(out=warm[:, 1:2], in_=warm[:, 0:1], func=ACT.Sin)
            nc.vector.memset(vectors[:], 0.0)
            nc.vector.memset(angle_rows[:], 0.0)
            for i, v in enumerate((bq, bk, gq, gk)):
                nc.scalar.dma_start(
                    out=vectors[HEADS * i : HEADS * (i + 1), :], in_=v.rearrange("(h c) -> h c", c=P)
                )
            nc.scalar.dma_start(out=angle_rows[0:FRAMES, 0:BY_FRAME], in_=theta[0:FRAMES, 0:BY_FRAME])
            nc.scalar.dma_start(
                out=angle_rows[ROW_H:ROW_W, BY_FRAME : BY_FRAME + BY_HEIGHT],
                in_=theta[0:HEIGHT, BY_FRAME : BY_FRAME + BY_HEIGHT],
            )
            nc.scalar.dma_start(
                out=angle_rows[ROW_W : ROW_W + WIDTH, BY_FRAME + BY_HEIGHT : PAIRS],
                in_=theta[0:WIDTH, BY_FRAME + BY_HEIGHT : PAIRS],
            )
            x_raw = {0: load_rows(x_rows, 0, 2, PASSES), 1: load_rows(x_rows, 2 * P, 2, 1)}
            wk_raw = {0: load_rows(wk, 0, 2), 1: load_rows(wk, 2 * P, 2)}
            nc.sync.dma_start(out=scale_rows[:], in_=wq_scale.rearrange("o k -> (o k)").partition_broadcast(P))
            load_bytes(0)
            load_bytes(1)
            make_identity(nc, ident_f32[:])

            picks = setup.tile([P, TOKENS], BF16, name="picks")
            nc.vector.memset(picks[:], 0.0)
            for pattern, first_row in (
                ([[1, FRAMES], [0, HEIGHT * WIDTH]], 0),
                ([[0, FRAMES], [1, HEIGHT], [0, WIDTH]], ROW_H),
                ([[0, FRAMES * HEIGHT], [1, WIDTH]], ROW_W),
            ):
                nc.gpsimd.affine_select(
                    out=picks[:],
                    in_=picks[:],
                    pattern=pattern,
                    compare_op=ALU.not_equal,
                    fill=1.0,
                    base=first_row,
                    channel_multiplier=-1,
                )
            make_identity(nc, ident_bf16[:])

            def make_trig():
                shifted = setup.tile([P, TOKEN_TILES * PAIRS], F32, name="shifted")
                folded = setup.tile([P, TOKEN_TILES * PAIRS], F32, name="folded")
                for lo, hi in ((0, 8), (8, TOKEN_TILES)):
                    angles = turn_psum.tile([P, 4 * P], F32, name="angles", tag="back")
                    for tile in range(lo, hi):
                        nc.tensor.matmul(
                            out=angles[:, (tile - lo) * PAIRS : (tile - lo + 1) * PAIRS],
                            lhsT=picks[:, tile * P : (tile + 1) * P],
                            rhs=angle_rows[:],
                            start=True,
                            stop=True,
                        )
                    nc.vector.tensor_scalar(
                        out=shifted[:, lo * PAIRS : hi * PAIRS],
                        in0=angles[:, 0 : (hi - lo) * PAIRS],
                        scalar1=math.pi,
                        scalar2=-PI_BELOW,
                        op0=ALU.subtract,
                        op1=ALU.max,
                    )
                nc.scalar.activation(out=folded[:], in_=shifted[:], func=ACT.Abs)
                for plane, (src, scale, bias) in enumerate(
                    ((folded, 1.0, -0.5 * math.pi), (shifted, 1.0, 0.0), (shifted, -1.0, 0.0))
                ):
                    nc.scalar.activation(
                        out=trig[:, :, plane * PAIRS : (plane + 1) * PAIRS],
                        in_=src[:].rearrange("p (t j) -> p t j", j=PAIRS),
                        func=ACT.Sin,
                        scale=scale,
                        bias=bias,
                    )

            nothing = (0, 0, 0)
            turn(x_raw[0], 2, x_codes, x_scales, 0, False, nothing)
            wk_raw[2] = load_rows(wk, 4 * P, 2)
            turn(x_raw[1], 2, x_codes, x_scales, 2 * P, False, nothing)
            wk_raw[3] = load_rows(wk, 6 * P, 2)
            turn(wk_raw[0], 2, w_codes[KEY], w_scales[KEY], 0, True, nothing)
            wk_raw[4] = load_rows(wk, 8 * P, 2)

            columns = turn_psum.tile([P, P], BF16, name="columns", tag="back")
            nc.tensor.transpose(columns[:], vectors[:], ident_bf16[:])
            nc.vector.tensor_copy(out=per_channel[:], in_=columns[:, 0 : 4 * HEADS])
            nc.vector.tensor_tensor(
                out=bias_gain[:],
                in0=per_channel[:, 0 : 2 * HEADS],
                in1=per_channel[:, 2 * HEADS : 4 * HEADS],
                op=ALU.mult,
            )

            for pair in range(ROW_PAIRS):
                if pair + 1 < ROW_PAIRS:
                    turn(wk_raw[pair + 1], 2, w_codes[KEY], w_scales[KEY], 2 * P * (pair + 1), True, WIDEN_BESIDE)
                else:
                    turn(x_raw[2], 2, x_codes, x_scales, 4 * P, True, WIDEN_BESIDE)
                if pair == 0:
                    wk_raw[5] = load_rows(wk, 10 * P, 2)
                elif pair == 1:
                    x_raw[2] = load_rows(x_rows, 4 * P, 2)
                elif pair == 2:
                    x_raw[3] = load_rows(x_rows, 6 * P, 2)
                elif pair == 3:
                    x_raw[4] = load_rows(x_rows, 8 * P, 1)
                project(0, 2 * pair)
                project(0, 2 * pair + 1)
                if pair == 0:
                    make_trig()
            turn(x_raw[3], 2, x_codes, x_scales, 6 * P, True, WIDEN_BESIDE)
            turn(x_raw[4], 1, x_codes, x_scales, 8 * P, True, WIDEN_BESIDE)

        first_unit[0] = False
        rope_pool = ctx.enter_context(tc.tile_pool(name="rope", bufs=4))
        small = ctx.enter_context(tc.tile_pool(name="small", bufs=3))

        scaled_trig = {}

        def norm(n, t):
            tile0 = UNITS[n][1]
            sums = turn_psum.tile([P, 4 * P], F32, name="sums", tag="back")
            for h in range(HEADS):
                nc.tensor.matmul(
                    out=sums[:, 0:P],
                    lhsT=squared[(n, h)][:, t * P : (t + 1) * P],
                    rhs=ident_f32[:],
                    is_transpose=True,
                    start=(h == 0),
                    stop=(h == HEADS - 1),
                )
            mean = small.tile([P, 1], F32, name="mean", tag="mean")
            rstd = small.tile([P, 1], F32, name="rstd", tag="rstd")
            unused = small.tile([P, P], F32, name="unused", tag="unused")
            nc.scalar.activation(
                out=unused[:], in_=sums[:, 0:P], func=ACT.Identity, scale=1.0 / CH, bias=EPS / P, accum_out=mean[:]
            )
            nc.scalar.activation(out=rstd[:], in_=mean[:], func=ACT.Abs_reciprocal_sqrt)
            scaled_trig[(n, t)] = small.tile(
                [P, 3 * PAIRS], F32, name="scaled_trig", tag="scaled_trig", bufs=8, align_bytes=256
            )
            nc.scalar.activation(out=scaled_trig[(n, t)][:], in_=trig[:, tile0 + t, :], func=ACT.Copy, scale=rstd[:])
            normed[0] += BANKS

        banks = []
        for n in range(len(UNITS)):
            for t in range(UNITS[n][2]):
                for b in range(BANKS):
                    banks.append((n, t, b))
        rotated = [0]
        normed = [0]
        added = [0]
        products = []

        def add_and_store():
            proj, tile, b, straight, crossed = products.pop(0)
            result = rope_pool.tile([P, 4 * P], F32, name="result", tag="result", bufs=6, align_bytes=256)
            if added[0] >= len(banks) - VECTOR_ADDS and added[0] % 2 == 1:
                nc.vector.tensor_tensor(out=result[:], in0=straight[:], in1=crossed[:], op=ALU.add)
            else:
                nc.gpsimd.tensor_tensor(out=result[:], in0=straight[:], in1=crossed[:], op=ALU.add)
            added[0] += 1
            nc.sync.dma_start(
                out=outs[proj][0, tile * P : (tile + 1) * P, BANK_HEADS * b : BANK_HEADS * (b + 1), :].rearrange(
                    "s h d -> s (h d)"
                ),
                in_=result[:],
            )

        def rotate(quota):
            for i in range(rotated[0], min(rotated[0] + quota, normed[0])):
                n, t, b = banks[i]
                back = back_psum.tile([P, 4 * P], F32, name="back", tag="back")
                for hh in range(BANK_HEADS):
                    nc.tensor.transpose(
                        back[:, hh * P : (hh + 1) * P],
                        gained[(n, BANK_HEADS * b + hh)][:, t * P : (t + 1) * P],
                        ident_f32[:],
                    )
                factors = scaled_trig[(n, t)]
                straight = rope_pool.tile([P, 4 * P], F32, name="straight", tag="straight", align_bytes=256)
                crossed = rope_pool.tile([P, 4 * P], F32, name="crossed", tag="crossed", align_bytes=256)
                nc.vector.tensor_tensor(
                    out=straight[:].rearrange("p (h j r) -> p h j r", h=BANK_HEADS, r=2),
                    in0=back[:].rearrange("p (h j r) -> p h j r", h=BANK_HEADS, r=2),
                    in1=factors[:, 0:PAIRS].unsqueeze(1).unsqueeze(3).to_broadcast([P, BANK_HEADS, PAIRS, 2]),
                    op=ALU.mult,
                )
                nc.vector.tensor_tensor(
                    out=crossed[:].rearrange("p (h j r) -> p h j r", h=BANK_HEADS, r=2),
                    in0=back[:].rearrange("p (h j r) -> p h j r", h=BANK_HEADS, r=2)[:, :, :, ::-1],
                    in1=factors[:, PAIRS : 3 * PAIRS]
                    .rearrange("p (r j) -> p j r", r=2)
                    .unsqueeze(1)
                    .to_broadcast([P, BANK_HEADS, PAIRS, 2]),
                    op=ALU.mult,
                )
                products.append((UNITS[n][0], UNITS[n][1] + t, b, straight, crossed))
                if len(products) > 1:
                    add_and_store()
                rotated[0] += 1

        wq_banks = PASSES * ROW_PAIRS
        wq_steps = 15
        wq_turned = 0
        pending = []
        step = 0
        for n in range(1, len(UNITS)):
            for s in range(STEPS):
                for h in range(STEP_HEADS * s, STEP_HEADS * (s + 1)):
                    project(n, h)
                rotate(ROPE_BANKS[s])
                if s % 2 == 0 and s // 2 < UNITS[n - 1][2]:
                    norm(n - 1, s // 2)
                step += 1
                due = min(wq_banks, (wq_banks * step + wq_steps - 1) // wq_steps)
                for i in range(wq_turned, due):
                    j, g = i // PASSES, i % PASSES
                    widen(max(0, 4 * (j + 1) - widened[0]))
                    pending.append(turn_bank(wq_wide[j], 2, g, w_codes[Q], w_scales[Q], 2 * P * j, False))
                    widen(1)
                    if len(pending) > 1:
                        quantise(pending.pop(0))
                wq_turned = due
                if due == wq_banks:
                    while pending:
                        quantise(pending.pop(0))
        rotate(len(banks))
        norm(len(UNITS) - 1, 0)
        rotate(len(banks))
        add_and_store()
